import numpy as np
import ml_dtypes


def mxq(x, axis, fmt="e4m3"):
    dtype, down = {"e4m3": (ml_dtypes.float8_e4m3fn, 7), "e5m2": (ml_dtypes.float8_e5m2, 14)}[fmt]
    v = np.moveaxis(np.asarray(x, np.float32).astype(ml_dtypes.bfloat16).astype(np.float64), axis, -1)
    blocks = v.reshape(v.shape[:-1] + (-1, 32))
    amax = np.abs(blocks).max(-1, keepdims=True)
    byte = np.maximum(np.where(amax > 0, np.frexp(amax)[1] - 1 + 127, 0) - down, 1)
    scale = np.exp2(byte - 127.0)
    codes = (blocks / scale).astype(np.float32).astype(dtype).astype(np.float64)
    return np.moveaxis((codes * scale).reshape(v.shape), -1, axis)


WIDE = False


def mx_kscale(k):
    if not WIDE:
        return np.ones(k)
    levels = np.array([10, -10, 5, -5, 0])
    a = np.random.permutation(np.resize(levels, k // 512 * 4)).reshape(k // 512, 4)
    idx = np.arange(k)
    return np.exp2(a[idx // 512, idx % 128 // 32])


BF16 = ml_dtypes.bfloat16


def bf(x):
    return np.asarray(x, np.float32).astype(BF16)


def f64(x):
    return np.asarray(x).astype(np.float64)


N, M, C, IMG = 4096, 1024, 512, 256
NEG = -1e9
MAX_DISP = 192.0
V_TOL = 3.0


def draw_kpts(n):
    return bf(np.stack([np.random.randint(0, IMG, n), np.random.randint(0, IMG, n)], axis=1))


def setup_inputs():
    t = mx_kscale(C)
    return {"Q": bf(np.random.standard_normal((N, C))),
            "K": bf(np.random.standard_normal((M, C))),
            "V": bf(np.random.standard_normal((M, C)) * t[None, :]),
            "kpts_L": draw_kpts(N),
            "kpts_R": draw_kpts(M),
            "Wm": bf(np.random.standard_normal((C, C)) / np.sqrt(C) / t[None, :]),
            "bm": bf(np.random.standard_normal(C) * 0.1)}


def reference(Q, K, V, kpts_L, kpts_R, Wm, bm):
    pl, pr = f64(kpts_L), f64(kpts_R)
    dist_v = np.abs(pl[:, 1:2] - pr[:, 1][None, :])
    dist_u = pl[:, 0:1] - pr[:, 0][None, :]
    mask = (dist_v < V_TOL) & (dist_u > 0) & (dist_u < MAX_DISP)
    attn = f64(Q) @ f64(K).T * (1.0 / np.sqrt(C))
    attn = np.where(mask, attn, NEG)
    e = np.exp(attn - attn.max(-1, keepdims=True))
    esum = e.sum(-1, keepdims=True)
    matched = (mxq(e, 1, "e4m3") @ mxq(f64(V), 0, "e4m3")) / esum
    return (mxq(matched, 1, "e4m3") @ mxq(f64(Wm), 1, "e4m3").T) + f64(bm)

@@ -1,0 +1,351 @@
+import math
+from contextlib import ExitStack
+
+import concourse.mybir as mybir
+from concourse.masks import make_identity
+
+BF16 = mybir.dt.bfloat16
+F32 = mybir.dt.float32
+U32 = mybir.dt.uint32
+U8 = mybir.dt.uint8
+FP8X4 = mybir.dt.float8_e4m3fn_x4
+ALU = mybir.AluOpType
+ACT = mybir.ActivationFunctionType
+
+P = 128
+PACK = 4
+QUERIES, KEYS, C = 4096, 1024, 512
+TILES = QUERIES // P
+KEY_TILES = KEYS // P
+C_TILES = C // P
+BANK = 512
+KEY_PASSES = KEYS // (P * PACK)
+
+FLOPS = 2 * QUERIES * KEYS * C * 2 + 2 * QUERIES * C * C
+
+BIG = 2.0**60
+V_TOL = 3.0
+U_HALF = 96.0
+V_STRETCH = U_HALF / V_TOL
+
+
+def tile_epipolarcrossattention_pa_t_kernel(tc, Q, K, V, kpts_L, kpts_R, Wm, bm, out):
+    nc = tc.nc
+    with ExitStack() as ctx:
+        ctx.enter_context(tc.manual_schedule())
+        const = ctx.enter_context(tc.tile_pool(name="const", bufs=1))
+        work = ctx.enter_context(tc.tile_pool(name="work", bufs=3))
+        psum = ctx.enter_context(tc.psum_pool(name="psum", bufs=1))
+
+        ident_bf = const.tile([P, P], BF16, name="ident_bf")
+        make_identity(nc, ident_bf[:])
+        ident_f32 = const.tile([P, P], F32, name="ident_f32")
+        make_identity(nc, ident_f32[:])
+
+        query_uv = const.tile([P, TILES, 2], BF16, name="query_uv")
+        nc.scalar.dma_start(out=query_uv[:], in_=kpts_L.rearrange("(p i) t -> p i t", i=TILES))
+        key_uv = const.tile([P, KEYS, 2], BF16, name="key_uv")
+        nc.scalar.dma_start(
+            out=key_uv[:].rearrange("p m t -> p (m t)"),
+            in_=kpts_R.rearrange("m t -> (m t)").partition_broadcast(P),
+        )
+        k_rows = const.tile([P, KEY_TILES, C], BF16, name="k_rows")
+        nc.sync.dma_start(out=k_rows[:], in_=K.rearrange("(j p) c -> p j c", p=P))
+        q_rows = const.tile([P, TILES, C], BF16, name="q_rows")
+        q_view = Q.rearrange("(p i) c -> p i c", i=TILES)
+        nc.sync.dma_start(out=q_rows[:, 0:2, :], in_=q_view[:, 0:2, :])
+        v_rows = const.tile([P, KEY_PASSES, PACK, C], BF16, name="v_rows")
+        nc.sync.dma_start(out=v_rows[:], in_=V.rearrange("(g p t) c -> p g t c", g=KEY_PASSES, t=PACK))
+        nc.sync.dma_start(out=q_rows[:, 2:4, :], in_=q_view[:, 2:4, :])
+        w_rows = const.tile([P, C_TILES, C], BF16, name="w_rows")
+        nc.sync.dma_start(out=w_rows[:], in_=Wm.rearrange("(a p) c -> p a c", p=P))
+        bias_row = const.tile([P, C], BF16, name="bias_row")
+        nc.sync.dma_start(out=bias_row[:], in_=bm.partition_broadcast(P))
+        for first in range(4, TILES, 4):
+            nc.sync.dma_start(out=q_rows[:, first : first + 4, :], in_=q_view[:, first : first + 4, :])
+
+        bias_v = const.tile([P, TILES], F32, name="bias_v")
+        nc.vector.tensor_scalar(
+            out=bias_v[:], in0=query_uv[:, :, 1], scalar1=-V_STRETCH * BIG, scalar2=None, op0=ALU.mult
+        )
+        bias_u = const.tile([P, TILES], F32, name="bias_u")
+        nc.vector.tensor_scalar(
+            out=bias_u[:], in0=query_uv[:, :, 0], scalar1=U_HALF, scalar2=-BIG, op0=ALU.subtract, op1=ALU.mult
+        )
+
+        kT = const.tile([P, C_TILES, KEYS], BF16, name="kT")
+        for j in range(KEY_TILES):
+            kt_ps = psum.tile([P, C_TILES, P], BF16, name="kt_ps", tag="scores", bufs=3)
+            for k in range(C_TILES):
+                nc.tensor.transpose(kt_ps[:, k, :], k_rows[:, j, k * P : (k + 1) * P], ident_bf[:])
+            if j % 2 == 0:
+                nc.vector.tensor_scalar(
+                    out=kT[:, :, j * P : (j + 1) * P], in0=kt_ps[:], scalar1=-1.0, scalar2=None, op0=ALU.mult
+                )
+            else:
+                nc.scalar.mul(out=kT[:, :, j * P : (j + 1) * P], in_=kt_ps[:], mul=-1.0)
+
+        v_codes = const.tile([P, KEY_PASSES, C], U32, name="v_codes", align_bytes=64)
+        v_scales = const.tile([P, KEY_PASSES, C], U8, name="v_scales", align_bytes=64)
+
+        def quantise_values():
+            v_grouped = const.tile([P, KEY_PASSES, C, PACK], BF16, name="v_grouped", align_bytes=64)
+            for g in range(KEY_PASSES):
+                nc.vector.tensor_copy(out=v_grouped[:, g], in_=v_rows[:, g].rearrange("p t c -> p c t"))
+            for g in range(KEY_PASSES):
+                nc.vector.quantize_mx(
+                    out=v_codes[:, g, :].bitcast(FP8X4),
+                    scales=v_scales[:, g, :],
+                    in_=v_grouped[:, g].rearrange("p c t -> p (c t)"),
+                )
+
+        w_codes = const.tile([P, C], U32, name="w_codes", align_bytes=64)
+        w_scales = const.tile([P, C], U8, name="w_scales", align_bytes=64)
+
+        def quantise_weights():
+            w_grouped = const.tile([P, C, PACK], BF16, name="w_grouped", align_bytes=64)
+            w_words = w_rows[:].bitcast(F32)
+            for a in range(C_TILES):
+                wt_ps = psum.tile([P, 2, P], F32, name="wt_ps", tag="tm")
+                for u in range(2):
+                    nc.tensor.transpose(wt_ps[:, u, :], w_words[:, a, u : C // 2 : 2], ident_f32[:])
+                nc.vector.tensor_copy(
+                    out=w_grouped[:].bitcast(F32)[:, a * P : (a + 1) * P, :],
+                    in_=wt_ps[:].rearrange("p u o -> p o u"),
+                )
+            nc.vector.quantize_mx(
+                out=w_codes[:].bitcast(FP8X4), scales=w_scales[:], in_=w_grouped[:].rearrange("p o t -> p (o t)")
+            )
+
+        out_view = out.rearrange("(p i) o -> p i o", i=TILES)
+        live = {}
+
+        def transpose_queries(i):
+            qt_ps = psum.tile([P, C_TILES, P], BF16, name="qt_ps", tag="tq")
+            for k in range(C_TILES):
+                nc.tensor.transpose(qt_ps[:, k, :], q_rows[:, i, k * P : (k + 1) * P], ident_bf[:])
+            live["qt_ps", i] = qt_ps
+
+        def copy_queries(i):
+            qT = work.tile([P, C_TILES, P], BF16, name="qT", tag="qT")
+            nc.vector.tensor_copy(out=qT[:], in_=live["qt_ps", i][:])
+            live["qT", i] = qT
+
+        def mask_distance_v(i):
+            far_v = work.tile([P, KEYS], BF16, name="far_v", tag="far_v")
+            nc.scalar.activation(
+                out=far_v[:], in_=key_uv[:, :, 1], func=ACT.Abs, scale=V_STRETCH * BIG, bias=bias_v[:, i : i + 1]
+            )
+            live["far_v", i] = far_v
+
+        def mask_distance_u(i):
+            far_u = work.tile([P, KEYS], BF16, name="far_u", tag="far_u")
+            nc.scalar.activation(
+                out=far_u[:], in_=key_uv[:, :, 0], func=ACT.Abs, scale=BIG, bias=bias_u[:, i : i + 1]
+            )
+            live["far_u", i] = far_u
+
+        def join_mask(i):
+            far = work.tile([P, KEYS], BF16, name="far", tag="far")
+            nc.vector.tensor_tensor(out=far[:], in0=live["far_v", i][:], in1=live["far_u", i][:], op=ALU.max)
+            live["far", i] = far
+
+        def scores(i, h):
+            s_ps = psum.tile([P, BANK], F32, name="s_ps", tag="scores", bufs=3)
+            for k in range(C_TILES):
+                nc.tensor.matmul(
+                    s_ps[:],
+                    lhsT=live["qT", i][:, k, :],
+                    rhs=kT[:, k, h * BANK : (h + 1) * BANK],
+                    start=(k == 0),
+                    stop=(k == C_TILES - 1),
+                )
+            live["s_ps", i, h] = s_ps
+
+        def mask_scores(i, h):
+            if h == 0:
+                live["neg", i] = work.tile([P, KEYS], F32, name="neg", tag="neg")
+            cols = slice(h * BANK, (h + 1) * BANK)
+            nc.vector.scalar_tensor_tensor(
+                out=live["neg", i][:, cols],
+                in0=live["far", i][:, cols],
+                scalar=(U_HALF - 0.5) * BIG,
+                in1=live["s_ps", i, h][:],
+                op0=ALU.subtract,
+                op1=ALU.max,
+            )
+
+        def row_minimum(i):
+            low = work.tile([P, 1], F32, name="low", tag="low")
+            nc.vector.tensor_reduce(out=low[:], in_=live["neg", i][:], axis=mybir.AxisListType.X, op=ALU.min)
+            live["low", i] = low
+
+        def exp_scale(i):
+            e_scale = work.tile([P, 1], F32, name="e_scale", tag="e_scale")
+            nc.vector.tensor_scalar(
+                out=e_scale[:],
+                in0=live["low", i][:],
+                scalar1=0.25 * BIG,
+                scalar2=-1.0 / math.sqrt(C),
+                op0=ALU.is_lt,
+                op1=ALU.mult,
+            )
+            live["e_scale", i] = e_scale
+
+        def exp_bias(i):
+            e_bias = work.tile([P, 1], F32, name="e_bias", tag="e_bias")
+            nc.vector.tensor_scalar(
+                out=e_bias[:],
+                in0=live["low", i][:],
+                scalar1=live["e_scale", i][:, 0:1],
+                scalar2=-1.0,
+                op0=ALU.mult,
+                op1=ALU.mult,
+            )
+            live["e_bias", i] = e_bias
+
+        def exponentials(i):
+            e_rows = work.tile([P, KEYS], BF16, name="e_rows", tag="e_rows")
+            e_sum = work.tile([P, 1], F32, name="e_sum", tag="e_sum")
+            nc.scalar.activation(
+                out=e_rows[:],
+                in_=live["neg", i][:],
+                func=ACT.Exp,
+                scale=live["e_scale", i][:, 0:1],
+                bias=live["e_bias", i][:, 0:1],
+                accum_out=e_sum[:, 0:1],
+            )
+            live["e_rows", i] = e_rows
+            live["e_sum", i] = e_sum
+
+        def invert_sum(i):
+            e_inv = work.tile([P, 1], F32, name="e_inv", tag="e_inv", bufs=4)
+            nc.vector.reciprocal(out=e_inv[:], in_=live["e_sum", i][:])
+            live["e_inv", i] = e_inv
+
+        def transpose_e(i):
+            e_words = live["e_rows", i][:].bitcast(F32)
+            et_ps = psum.tile([P, KEY_PASSES, 2, P], F32, name="et_ps", tag="te")
+            for g in range(KEY_PASSES):
+                for u in range(2):
+                    nc.tensor.transpose(
+                        et_ps[:, g, u, :], e_words[:, g * 2 * P + u : (g + 1) * 2 * P : 2], ident_f32[:]
+                    )
+            live["et_ps", i] = et_ps
+
+        def copy_e(i):
+            e_grouped = work.tile([P, KEY_PASSES, P, PACK], BF16, name="e_grouped", tag="e_grouped", align_bytes=64)
+            nc.scalar.copy(out=e_grouped[:].bitcast(F32), in_=live["et_ps", i][:].rearrange("p g u n -> p g n u"))
+            live["e_grouped", i] = e_grouped
+
+        def quantise_e(i):
+            e_codes = work.tile([P, KEY_PASSES, P], U32, name="e_codes", tag="e_codes", align_bytes=64)
+            e_scales = work.tile([P, KEY_PASSES, P], U8, name="e_scales", tag="e_scales", align_bytes=64)
+            nc.vector.quantize_mx(
+                out=e_codes[:].rearrange("p g n -> p (g n)").bitcast(FP8X4),
+                scales=e_scales[:].rearrange("p g n -> p (g n)"),
+                in_=live["e_grouped", i][:].rearrange("p g n t -> p (g n t)"),
+            )
+            live["e_codes", i] = e_codes
+            live["e_scales", i] = e_scales
+
+        def weighted_sum(i):
+            pv_ps = psum.tile([P, C], F32, name="pv_ps", tag="pv")
+            for g in range(KEY_PASSES):
+                nc.tensor.matmul_mx(
+                    out=pv_ps[:],
+                    lhsT=live["e_codes", i][:, g, :].bitcast(FP8X4),
+                    lhsT_scale=live["e_scales", i][:, g, :],
+                    rhs=v_codes[:, g, :].bitcast(FP8X4),
+                    rhs_scale=v_scales[:, g, :],
+                    start=(g == 0),
+                    stop=(g == KEY_PASSES - 1),
+                )
+            live["pv_ps", i] = pv_ps
+
+        def normalise(i):
+            matched = work.tile([P, C], BF16, name="matched", tag="matched")
+            nc.scalar.activation(
+                out=matched[:], in_=live["pv_ps", i][:], func=ACT.Copy, scale=live["e_inv", i][:, 0:1]
+            )
+            live["matched", i] = matched
+
+        def transpose_matched(i):
+            m_words = live["matched", i][:].bitcast(F32)
+            mt_ps = psum.tile([P, 2, P], F32, name="mt_ps", tag="tm")
+            for u in range(2):
+                nc.tensor.transpose(mt_ps[:, u, :], m_words[:, u : C // 2 : 2], ident_f32[:])
+            live["mt_ps", i] = mt_ps
+
+        def copy_matched(i):
+            m_grouped = work.tile([P, P, PACK], BF16, name="m_grouped", tag="m_grouped", align_bytes=64)
+            nc.vector.tensor_copy(out=m_grouped[:].bitcast(F32), in_=live["mt_ps", i][:].rearrange("p u n -> p n u"))
+            live["m_grouped", i] = m_grouped
+
+        def quantise_matched(i):
+            m_codes = work.tile([P, P], U32, name="m_codes", tag="m_codes", align_bytes=64)
+            m_scales = work.tile([P, P], U8, name="m_scales", tag="m_scales", align_bytes=64)
+            nc.vector.quantize_mx(
+                out=m_codes[:].bitcast(FP8X4),
+                scales=m_scales[:],
+                in_=live["m_grouped", i][:].rearrange("p n t -> p (n t)"),
+            )
+            live["m_codes", i] = m_codes
+            live["m_scales", i] = m_scales
+
+        def project(i):
+            o_ps = psum.tile([P, C], F32, name="o_ps", tag="fo")
+            nc.tensor.matmul_mx(
+                out=o_ps[:],
+                lhsT=live["m_codes", i][:].bitcast(FP8X4),
+                lhsT_scale=live["m_scales", i][:],
+                rhs=w_codes[:].bitcast(FP8X4),
+                rhs_scale=w_scales[:],
+                start=True,
+                stop=True,
+            )
+            live["o_ps", i] = o_ps
+
+        def add_bias_and_store(i):
+            o_rows = work.tile([P, C], F32, name="o_rows", tag="o_rows", bufs=4)
+            nc.vector.tensor_tensor(out=o_rows[:], in0=live["o_ps", i][:], in1=bias_row[:], op=ALU.add)
+            nc.sync.dma_start(out=out_view[:, i, :], in_=o_rows[:])
+
+        def on_tile(stage, i, *args):
+            if 0 <= i < TILES:
+                stage(i, *args)
+
+        def step(k):
+            on_tile(transpose_e, k - 1)
+            on_tile(transpose_matched, k - 3)
+            on_tile(transpose_queries, k + 2)
+            on_tile(mask_scores, k, 1)
+            on_tile(quantise_matched, k - 4)
+            on_tile(invert_sum, k - 1)
+            on_tile(row_minimum, k)
+            on_tile(copy_e, k - 1)
+            on_tile(mask_distance_v, k + 3)
+            on_tile(scores, k + 1, 0)
+            on_tile(copy_matched, k - 3)
+            on_tile(exp_scale, k)
+            on_tile(copy_queries, k + 2)
+            on_tile(exp_bias, k)
+            on_tile(exponentials, k)
+            on_tile(quantise_e, k - 1)
+            on_tile(weighted_sum, k - 2)
+            on_tile(project, k - 4)
+            on_tile(mask_scores, k + 1, 0)
+            on_tile(normalise, k - 2)
+            on_tile(mask_distance_u, k + 3)
+            on_tile(scores, k + 1, 1)
+            on_tile(add_bias_and_store, k - 4)
+            on_tile(join_mask, k + 2)
+
+        step(-3)
+        step(-2)
+        quantise_values()
+        step(-1)
+        step(0)
+        quantise_weights()
+        for k in range(1, TILES + 4):
+            step(k)

@@ -8,6 +8,7 @@ BF16 = mybir.dt.bfloat16
 F32 = mybir.dt.float32
 U32 = mybir.dt.uint32
 U8 = mybir.dt.uint8
+I32 = mybir.dt.int32
 FP8X4 = mybir.dt.float8_e4m3fn_x4
 ALU = mybir.AluOpType
 ACT = mybir.ActivationFunctionType
@@ -50,7 +51,9 @@ def tile_epipolarcrossattention_pa_t_kernel(tc, Q, K, V, kpts_L, kpts_R, Wm, bm,
             in_=kpts_R.rearrange("m t -> (m t)").partition_broadcast(P),
         )
         k_rows = const.tile([P, KEY_TILES, C], BF16, name="k_rows")
-        nc.sync.dma_start(out=k_rows[:], in_=K.rearrange("(j p) c -> p j c", p=P))
+        k_view = K.rearrange("(j p) c -> p j c", p=P)
+        nc.sync.dma_start(out=k_rows[:, 0:4, :], in_=k_view[:, 0:4, :])
+        nc.sync.dma_start(out=k_rows[:, 4:8, :], in_=k_view[:, 4:8, :])
         q_rows = const.tile([P, TILES, C], BF16, name="q_rows")
         q_view = Q.rearrange("(p i) c -> p i c", i=TILES)
         nc.sync.dma_start(out=q_rows[:, 0:2, :], in_=q_view[:, 0:2, :])
@@ -64,10 +67,10 @@ def tile_epipolarcrossattention_pa_t_kernel(tc, Q, K, V, kpts_L, kpts_R, Wm, bm,
         for first in range(4, TILES, 4):
             nc.sync.dma_start(out=q_rows[:, first : first + 4, :], in_=q_view[:, first : first + 4, :])
 
-        bias_v = const.tile([P, TILES], F32, name="bias_v")
-        nc.vector.tensor_scalar(
-            out=bias_v[:], in0=query_uv[:, :, 1], scalar1=-V_STRETCH * BIG, scalar2=None, op0=ALU.mult
-        )
+        query_v = const.tile([P, TILES], F32, name="query_v")
+        nc.vector.tensor_copy(out=query_v[:], in_=query_uv[:, :, 1])
+        key_v = const.tile([P, KEYS], BF16, name="key_v")
+        nc.vector.tensor_copy(out=key_v[:], in_=key_uv[:, :, 1])
         bias_u = const.tile([P, TILES], F32, name="bias_u")
         nc.vector.tensor_scalar(
             out=bias_u[:], in0=query_uv[:, :, 0], scalar1=U_HALF, scalar2=-BIG, op0=ALU.subtract, op1=ALU.mult
@@ -78,20 +81,25 @@ def tile_epipolarcrossattention_pa_t_kernel(tc, Q, K, V, kpts_L, kpts_R, Wm, bm,
             kt_ps = psum.tile([P, C_TILES, P], BF16, name="kt_ps", tag="scores", bufs=3)
             for k in range(C_TILES):
                 nc.tensor.transpose(kt_ps[:, k, :], k_rows[:, j, k * P : (k + 1) * P], ident_bf[:])
-            if j % 2 == 0:
-                nc.vector.tensor_scalar(
-                    out=kT[:, :, j * P : (j + 1) * P], in0=kt_ps[:], scalar1=-1.0, scalar2=None, op0=ALU.mult
-                )
-            else:
-                nc.scalar.mul(out=kT[:, :, j * P : (j + 1) * P], in_=kt_ps[:], mul=-1.0)
+            nc.vector.tensor_scalar(
+                out=kT[:, :, j * P : (j + 1) * P], in0=kt_ps[:], scalar1=-1.0, scalar2=None, op0=ALU.mult
+            )
 
         v_codes = const.tile([P, KEY_PASSES, C], U32, name="v_codes", align_bytes=64)
         v_scales = const.tile([P, KEY_PASSES, C], U8, name="v_scales", align_bytes=64)
 
+        v_grouped = const.tile([P, KEY_PASSES, C, PACK], BF16, name="v_grouped", align_bytes=64)
+        for g in range(KEY_PASSES):
+            nc.gpsimd.tensor_scalar(
+                out=v_grouped[:, g],
+                in0=v_rows[:, g].rearrange("p t c -> p c t"),
+                scalar1=1.0,
+                scalar2=0.0,
+                op0=ALU.mult,
+                op1=ALU.add,
+            )
+
         def quantise_values():
-            v_grouped = const.tile([P, KEY_PASSES, C, PACK], BF16, name="v_grouped", align_bytes=64)
-            for g in range(KEY_PASSES):
-                nc.vector.tensor_copy(out=v_grouped[:, g], in_=v_rows[:, g].rearrange("p t c -> p c t"))
             for g in range(KEY_PASSES):
                 nc.vector.quantize_mx(
                     out=v_codes[:, g, :].bitcast(FP8X4),
@@ -109,7 +117,7 @@ def tile_epipolarcrossattention_pa_t_kernel(tc, Q, K, V, kpts_L, kpts_R, Wm, bm,
                 wt_ps = psum.tile([P, 2, P], F32, name="wt_ps", tag="tm")
                 for u in range(2):
                     nc.tensor.transpose(wt_ps[:, u, :], w_words[:, a, u : C // 2 : 2], ident_f32[:])
-                nc.vector.tensor_copy(
+                nc.scalar.copy(
                     out=w_grouped[:].bitcast(F32)[:, a * P : (a + 1) * P, :],
                     in_=wt_ps[:].rearrange("p u o -> p o u"),
                 )
@@ -128,13 +136,29 @@ def tile_epipolarcrossattention_pa_t_kernel(tc, Q, K, V, kpts_L, kpts_R, Wm, bm,
 
         def copy_queries(i):
             qT = work.tile([P, C_TILES, P], BF16, name="qT", tag="qT")
-            nc.vector.tensor_copy(out=qT[:], in_=live["qt_ps", i][:])
+            nc.scalar.copy(out=qT[:], in_=live["qt_ps", i][:])
             live["qT", i] = qT
+
+        def mask_offset_v(i):
+            off_v = work.tile([P, KEYS], BF16, name="off_v", tag="off_v")
+            nc.vector.tensor_scalar(
+                out=off_v[:],
+                in0=key_v[:],
+                scalar1=query_v[:, i : i + 1],
+                scalar2=V_STRETCH * BIG,
+                op0=ALU.subtract,
+                op1=ALU.mult,
+            )
+            live["off_v", i] = off_v
 
         def mask_distance_v(i):
             far_v = work.tile([P, KEYS], BF16, name="far_v", tag="far_v")
-            nc.scalar.activation(
-                out=far_v[:], in_=key_uv[:, :, 1], func=ACT.Abs, scale=V_STRETCH * BIG, bias=bias_v[:, i : i + 1]
+            nc.vector.tensor_scalar(
+                out=far_v[:].bitcast(I32),
+                in0=live["off_v", i][:].bitcast(I32),
+                scalar1=0x7FFF7FFF,
+                scalar2=None,
+                op0=ALU.bitwise_and,
             )
             live["far_v", i] = far_v
 
@@ -164,7 +188,7 @@ def tile_epipolarcrossattention_pa_t_kernel(tc, Q, K, V, kpts_L, kpts_R, Wm, bm,
 
         def mask_scores(i, h):
             if h == 0:
-                live["neg", i] = work.tile([P, KEYS], F32, name="neg", tag="neg")
+                live["neg", i] = work.tile([P, KEYS], F32, name="neg", tag="neg", bufs=4)
             cols = slice(h * BANK, (h + 1) * BANK)
             nc.vector.scalar_tensor_tensor(
                 out=live["neg", i][:, cols],
@@ -182,7 +206,7 @@ def tile_epipolarcrossattention_pa_t_kernel(tc, Q, K, V, kpts_L, kpts_R, Wm, bm,
 
         def exp_scale(i):
             e_scale = work.tile([P, 1], F32, name="e_scale", tag="e_scale")
-            nc.vector.tensor_scalar(
+            nc.gpsimd.tensor_scalar(
                 out=e_scale[:],
                 in0=live["low", i][:],
                 scalar1=0.25 * BIG,
@@ -194,7 +218,7 @@ def tile_epipolarcrossattention_pa_t_kernel(tc, Q, K, V, kpts_L, kpts_R, Wm, bm,
 
         def exp_bias(i):
             e_bias = work.tile([P, 1], F32, name="e_bias", tag="e_bias")
-            nc.vector.tensor_scalar(
+            nc.gpsimd.tensor_scalar(
                 out=e_bias[:],
                 in0=live["low", i][:],
                 scalar1=live["e_scale", i][:, 0:1],
@@ -279,7 +303,7 @@ def tile_epipolarcrossattention_pa_t_kernel(tc, Q, K, V, kpts_L, kpts_R, Wm, bm,
 
         def copy_matched(i):
             m_grouped = work.tile([P, P, PACK], BF16, name="m_grouped", tag="m_grouped", align_bytes=64)
-            nc.vector.tensor_copy(out=m_grouped[:].bitcast(F32), in_=live["mt_ps", i][:].rearrange("p u n -> p n u"))
+            nc.scalar.copy(out=m_grouped[:].bitcast(F32), in_=live["mt_ps", i][:].rearrange("p u n -> p n u"))
             live["m_grouped", i] = m_grouped
 
         def quantise_matched(i):
@@ -316,36 +340,37 @@ def tile_epipolarcrossattention_pa_t_kernel(tc, Q, K, V, kpts_L, kpts_R, Wm, bm,
                 stage(i, *args)
 
         def step(k):
-            on_tile(transpose_e, k - 1)
-            on_tile(transpose_matched, k - 3)
+            on_tile(transpose_e, k - 2)
+            on_tile(transpose_matched, k - 5)
             on_tile(transpose_queries, k + 2)
+            on_tile(exponentials, k - 1)
+            on_tile(normalise, k - 4)
             on_tile(mask_scores, k, 1)
-            on_tile(quantise_matched, k - 4)
-            on_tile(invert_sum, k - 1)
+            on_tile(join_mask, k + 1)
+            on_tile(add_bias_and_store, k - 7)
+            on_tile(quantise_matched, k - 6)
             on_tile(row_minimum, k)
-            on_tile(copy_e, k - 1)
-            on_tile(mask_distance_v, k + 3)
-            on_tile(scores, k + 1, 0)
-            on_tile(copy_matched, k - 3)
             on_tile(exp_scale, k)
-            on_tile(copy_queries, k + 2)
             on_tile(exp_bias, k)
-            on_tile(exponentials, k)
-            on_tile(quantise_e, k - 1)
-            on_tile(weighted_sum, k - 2)
-            on_tile(project, k - 4)
-            on_tile(mask_scores, k + 1, 0)
-            on_tile(normalise, k - 2)
+            on_tile(copy_e, k - 2)
+            on_tile(copy_matched, k - 5)
+            on_tile(copy_queries, k + 2)
+            on_tile(scores, k + 1, 0)
+            on_tile(invert_sum, k - 2)
+            on_tile(mask_offset_v, k + 2)
+            on_tile(quantise_e, k - 2)
             on_tile(mask_distance_u, k + 3)
+            on_tile(weighted_sum, k - 3)
+            on_tile(project, k - 6)
+            on_tile(mask_scores, k + 1, 0)
+            on_tile(mask_distance_v, k + 2)
             on_tile(scores, k + 1, 1)
-            on_tile(add_bias_and_store, k - 4)
-            on_tile(join_mask, k + 2)
 
         step(-3)
         step(-2)
-        quantise_values()
         step(-1)
         step(0)
+        quantise_values()
         quantise_weights()
-        for k in range(1, TILES + 4):
+        for k in range(1, TILES + 7):
             step(k)

@@ -24,10 +24,13 @@ KEY_PASSES = KEYS // (P * PACK)
 
 FLOPS = 2 * QUERIES * KEYS * C * 2 + 2 * QUERIES * C * C
 
-BIG = 2.0**60
-V_TOL = 3.0
+FAR = 512.0
 U_HALF = 96.0
-V_STRETCH = U_HALF / V_TOL
+V_STRETCH = 192.0
+U_STRETCH = 5.375
+
+TINY = 2.0**-80
+E_SCALE = 1.0 / (TINY * math.sqrt(C))
 
 
 def tile_epipolarcrossattention_pa_t_kernel(tc, Q, K, V, kpts_L, kpts_R, Wm, bm, out):
@@ -73,7 +76,7 @@ def tile_epipolarcrossattention_pa_t_kernel(tc, Q, K, V, kpts_L, kpts_R, Wm, bm,
         nc.vector.tensor_copy(out=key_v[:], in_=key_uv[:, :, 1])
         bias_u = const.tile([P, TILES], F32, name="bias_u")
         nc.vector.tensor_scalar(
-            out=bias_u[:], in0=query_uv[:, :, 0], scalar1=U_HALF, scalar2=-BIG, op0=ALU.subtract, op1=ALU.mult
+            out=bias_u[:], in0=query_uv[:, :, 0], scalar1=U_HALF, scalar2=-U_STRETCH, op0=ALU.subtract, op1=ALU.mult
         )
 
         kT = const.tile([P, C_TILES, KEYS], BF16, name="kT")
@@ -82,7 +85,7 @@ def tile_epipolarcrossattention_pa_t_kernel(tc, Q, K, V, kpts_L, kpts_R, Wm, bm,
             for k in range(C_TILES):
                 nc.tensor.transpose(kt_ps[:, k, :], k_rows[:, j, k * P : (k + 1) * P], ident_bf[:])
             nc.vector.tensor_scalar(
-                out=kT[:, :, j * P : (j + 1) * P], in0=kt_ps[:], scalar1=-1.0, scalar2=None, op0=ALU.mult
+                out=kT[:, :, j * P : (j + 1) * P], in0=kt_ps[:], scalar1=TINY, scalar2=None, op0=ALU.mult
             )
 
         v_codes = const.tile([P, KEY_PASSES, C], U32, name="v_codes", align_bytes=64)
@@ -145,33 +148,29 @@ def tile_epipolarcrossattention_pa_t_kernel(tc, Q, K, V, kpts_L, kpts_R, Wm, bm,
                 out=off_v[:],
                 in0=key_v[:],
                 scalar1=query_v[:, i : i + 1],
-                scalar2=V_STRETCH * BIG,
+                scalar2=V_STRETCH,
                 op0=ALU.subtract,
                 op1=ALU.mult,
             )
             live["off_v", i] = off_v
 
-        def mask_distance_v(i):
-            far_v = work.tile([P, KEYS], BF16, name="far_v", tag="far_v")
-            nc.vector.tensor_scalar(
-                out=far_v[:].bitcast(I32),
-                in0=live["off_v", i][:].bitcast(I32),
-                scalar1=0x7FFF7FFF,
-                scalar2=None,
-                op0=ALU.bitwise_and,
-            )
-            live["far_v", i] = far_v
-
         def mask_distance_u(i):
             far_u = work.tile([P, KEYS], BF16, name="far_u", tag="far_u")
             nc.scalar.activation(
-                out=far_u[:], in_=key_uv[:, :, 0], func=ACT.Abs, scale=BIG, bias=bias_u[:, i : i + 1]
+                out=far_u[:], in_=key_uv[:, :, 0], func=ACT.Abs, scale=U_STRETCH, bias=bias_u[:, i : i + 1]
             )
             live["far_u", i] = far_u
 
         def join_mask(i):
             far = work.tile([P, KEYS], BF16, name="far", tag="far")
-            nc.vector.tensor_tensor(out=far[:], in0=live["far_v", i][:], in1=live["far_u", i][:], op=ALU.max)
+            nc.vector.scalar_tensor_tensor(
+                out=far[:].bitcast(I32),
+                in0=live["off_v", i][:].bitcast(I32),
+                scalar=0x7FFF7FFF,
+                in1=live["far_u", i][:].bitcast(I32),
+                op0=ALU.bitwise_and,
+                op1=ALU.bitwise_or,
+            )
             live["far", i] = far
 
         def scores(i, h):
@@ -193,10 +192,10 @@ def tile_epipolarcrossattention_pa_t_kernel(tc, Q, K, V, kpts_L, kpts_R, Wm, bm,
             nc.vector.scalar_tensor_tensor(
                 out=live["neg", i][:, cols],
                 in0=live["far", i][:, cols],
-                scalar=(U_HALF - 0.5) * BIG,
+                scalar=FAR,
                 in1=live["s_ps", i, h][:],
-                op0=ALU.subtract,
-                op1=ALU.max,
+                op0=ALU.is_ge,
+                op1=ALU.subtract,
             )
 
         def row_minimum(i):
@@ -204,25 +203,13 @@ def tile_epipolarcrossattention_pa_t_kernel(tc, Q, K, V, kpts_L, kpts_R, Wm, bm,
             nc.vector.tensor_reduce(out=low[:], in_=live["neg", i][:], axis=mybir.AxisListType.X, op=ALU.min)
             live["low", i] = low
 
-        def exp_scale(i):
-            e_scale = work.tile([P, 1], F32, name="e_scale", tag="e_scale")
-            nc.gpsimd.tensor_scalar(
-                out=e_scale[:],
-                in0=live["low", i][:],
-                scalar1=0.25 * BIG,
-                scalar2=-1.0 / math.sqrt(C),
-                op0=ALU.is_lt,
-                op1=ALU.mult,
-            )
-            live["e_scale", i] = e_scale
-
         def exp_bias(i):
             e_bias = work.tile([P, 1], F32, name="e_bias", tag="e_bias")
             nc.gpsimd.tensor_scalar(
                 out=e_bias[:],
                 in0=live["low", i][:],
-                scalar1=live["e_scale", i][:, 0:1],
-                scalar2=-1.0,
+                scalar1=E_SCALE,
+                scalar2=1.0,
                 op0=ALU.mult,
                 op1=ALU.mult,
             )
@@ -235,7 +222,7 @@ def tile_epipolarcrossattention_pa_t_kernel(tc, Q, K, V, kpts_L, kpts_R, Wm, bm,
                 out=e_rows[:],
                 in_=live["neg", i][:],
                 func=ACT.Exp,
-                scale=live["e_scale", i][:, 0:1],
+                scale=-E_SCALE,
                 bias=live["e_bias", i][:, 0:1],
                 accum_out=e_sum[:, 0:1],
             )
@@ -350,7 +337,6 @@ def tile_epipolarcrossattention_pa_t_kernel(tc, Q, K, V, kpts_L, kpts_R, Wm, bm,
             on_tile(add_bias_and_store, k - 7)
             on_tile(quantise_matched, k - 6)
             on_tile(row_minimum, k)
-            on_tile(exp_scale, k)
             on_tile(exp_bias, k)
             on_tile(copy_e, k - 2)
             on_tile(copy_matched, k - 5)
@@ -363,7 +349,6 @@ def tile_epipolarcrossattention_pa_t_kernel(tc, Q, K, V, kpts_L, kpts_R, Wm, bm,
             on_tile(weighted_sum, k - 3)
             on_tile(project, k - 6)
             on_tile(mask_scores, k + 1, 0)
-            on_tile(mask_distance_v, k + 2)
             on_tile(scores, k + 1, 1)
 
         step(-3)

@@ -41,8 +41,6 @@ def tile_epipolarcrossattention_pa_t_kernel(tc, Q, K, V, kpts_L, kpts_R, Wm, bm,
         work = ctx.enter_context(tc.tile_pool(name="work", bufs=3))
         psum = ctx.enter_context(tc.psum_pool(name="psum", bufs=1))
 
-        ident_bf = const.tile([P, P], BF16, name="ident_bf")
-        make_identity(nc, ident_bf[:])
         ident_f32 = const.tile([P, P], F32, name="ident_f32")
         make_identity(nc, ident_f32[:])
 
@@ -61,7 +59,11 @@ def tile_epipolarcrossattention_pa_t_kernel(tc, Q, K, V, kpts_L, kpts_R, Wm, bm,
         q_view = Q.rearrange("(p i) c -> p i c", i=TILES)
         nc.sync.dma_start(out=q_rows[:, 0:2, :], in_=q_view[:, 0:2, :])
         v_rows = const.tile([P, KEY_PASSES, PACK, C], BF16, name="v_rows")
-        nc.sync.dma_start(out=v_rows[:], in_=V.rearrange("(g p t) c -> p g t c", g=KEY_PASSES, t=PACK))
+        for g in range(KEY_PASSES):
+            nc.sync.dma_start(
+                out=v_rows[:, g].rearrange("p (u e) c -> p u (e c)", e=2),
+                in_=V[g * P * PACK : (g + 1) * P * PACK, :].rearrange("(u p e) c -> p u (e c)", u=2, e=2),
+            )
         nc.sync.dma_start(out=q_rows[:, 2:4, :], in_=q_view[:, 2:4, :])
         w_rows = const.tile([P, C_TILES, C], BF16, name="w_rows")
         nc.sync.dma_start(out=w_rows[:], in_=Wm.rearrange("(a p) c -> p a c", p=P))
@@ -70,8 +72,8 @@ def tile_epipolarcrossattention_pa_t_kernel(tc, Q, K, V, kpts_L, kpts_R, Wm, bm,
         for first in range(4, TILES, 4):
             nc.sync.dma_start(out=q_rows[:, first : first + 4, :], in_=q_view[:, first : first + 4, :])
 
-        query_v = const.tile([P, TILES], F32, name="query_v")
-        nc.vector.tensor_copy(out=query_v[:], in_=query_uv[:, :, 1])
+        bias_v = const.tile([P, TILES], F32, name="bias_v")
+        nc.vector.tensor_scalar(out=bias_v[:], in0=query_uv[:, :, 1], scalar1=-1.0, scalar2=None, op0=ALU.mult)
         key_v = const.tile([P, KEYS], BF16, name="key_v")
         nc.vector.tensor_copy(out=key_v[:], in_=key_uv[:, :, 1])
         bias_u = const.tile([P, TILES], F32, name="bias_u")
@@ -79,23 +81,30 @@ def tile_epipolarcrossattention_pa_t_kernel(tc, Q, K, V, kpts_L, kpts_R, Wm, bm,
             out=bias_u[:], in0=query_uv[:, :, 0], scalar1=U_HALF, scalar2=-U_STRETCH, op0=ALU.subtract, op1=ALU.mult
         )
 
-        kT = const.tile([P, C_TILES, KEYS], BF16, name="kT")
+        kT = const.tile([P, 2, 2, KEYS], BF16, name="kT")
+        k_words = k_rows[:].bitcast(F32)
         for j in range(KEY_TILES):
-            kt_ps = psum.tile([P, C_TILES, P], BF16, name="kt_ps", tag="scores", bufs=3)
-            for k in range(C_TILES):
-                nc.tensor.transpose(kt_ps[:, k, :], k_rows[:, j, k * P : (k + 1) * P], ident_bf[:])
+            kt_ps = psum.tile([P, 2, P], F32, name="kt_ps", tag="scores", bufs=3)
+            for u in range(2):
+                nc.tensor.transpose(kt_ps[:, u, :], k_words[:, j, u * P : (u + 1) * P], ident_f32[:])
             nc.vector.tensor_scalar(
-                out=kT[:, :, j * P : (j + 1) * P], in0=kt_ps[:], scalar1=TINY, scalar2=None, op0=ALU.mult
+                out=kT[:, :, :, j * P : (j + 1) * P],
+                in0=kt_ps[:].bitcast(BF16).rearrange("p u (m e) -> p u e m", e=2),
+                scalar1=TINY,
+                scalar2=None,
+                op0=ALU.mult,
             )
 
         v_codes = const.tile([P, KEY_PASSES, C], U32, name="v_codes", align_bytes=64)
         v_scales = const.tile([P, KEY_PASSES, C], U8, name="v_scales", align_bytes=64)
 
         v_grouped = const.tile([P, KEY_PASSES, C, PACK], BF16, name="v_grouped", align_bytes=64)
-        for g in range(KEY_PASSES):
+
+        def group_values(g, half):
+            cols = slice(half * C // 2, (half + 1) * C // 2)
             nc.gpsimd.tensor_scalar(
-                out=v_grouped[:, g],
-                in0=v_rows[:, g].rearrange("p t c -> p c t"),
+                out=v_grouped[:, g, cols, :],
+                in0=v_rows[:, g, :, cols].rearrange("p t c -> p c t"),
                 scalar1=1.0,
                 scalar2=0.0,
                 op0=ALU.mult,
@@ -117,9 +126,9 @@ def tile_epipolarcrossattention_pa_t_kernel(tc, Q, K, V, kpts_L, kpts_R, Wm, bm,
             w_grouped = const.tile([P, C, PACK], BF16, name="w_grouped", align_bytes=64)
             w_words = w_rows[:].bitcast(F32)
             for a in range(C_TILES):
-                wt_ps = psum.tile([P, 2, P], F32, name="wt_ps", tag="tm")
+                wt_ps = psum.tile([P, 2, P], F32, name="wt_ps", tag="fo", bufs=2)
                 for u in range(2):
-                    nc.tensor.transpose(wt_ps[:, u, :], w_words[:, a, u : C // 2 : 2], ident_f32[:])
+                    nc.tensor.transpose(wt_ps[:, u, :], w_words[:, a, u * P : (u + 1) * P], ident_f32[:])
                 nc.scalar.copy(
                     out=w_grouped[:].bitcast(F32)[:, a * P : (a + 1) * P, :],
                     in_=wt_ps[:].rearrange("p u o -> p o u"),
@@ -131,25 +140,19 @@ def tile_epipolarcrossattention_pa_t_kernel(tc, Q, K, V, kpts_L, kpts_R, Wm, bm,
         out_view = out.rearrange("(p i) o -> p i o", i=TILES)
         live = {}
 
-        def transpose_queries(i):
-            qt_ps = psum.tile([P, C_TILES, P], BF16, name="qt_ps", tag="tq")
-            for k in range(C_TILES):
-                nc.tensor.transpose(qt_ps[:, k, :], q_rows[:, i, k * P : (k + 1) * P], ident_bf[:])
-            live["qt_ps", i] = qt_ps
-
-        def copy_queries(i):
-            qT = work.tile([P, C_TILES, P], BF16, name="qT", tag="qT")
-            nc.scalar.copy(out=qT[:], in_=live["qt_ps", i][:])
-            live["qT", i] = qT
+        def transpose_queries(i, t_ps):
+            q_words = q_rows[:].bitcast(F32)
+            for u in range(2):
+                nc.tensor.transpose(t_ps[:, 0, u, :], q_words[:, i, u * P : (u + 1) * P], ident_f32[:])
 
         def mask_offset_v(i):
-            off_v = work.tile([P, KEYS], BF16, name="off_v", tag="off_v")
-            nc.vector.tensor_scalar(
+            off_v = work.tile([P, KEYS], BF16, name="off_v", tag="off_v", bufs=2)
+            nc.gpsimd.tensor_scalar(
                 out=off_v[:],
                 in0=key_v[:],
-                scalar1=query_v[:, i : i + 1],
+                scalar1=bias_v[:, i : i + 1],
                 scalar2=V_STRETCH,
-                op0=ALU.subtract,
+                op0=ALU.add,
                 op1=ALU.mult,
             )
             live["off_v", i] = off_v
@@ -178,8 +181,8 @@ def tile_epipolarcrossattention_pa_t_kernel(tc, Q, K, V, kpts_L, kpts_R, Wm, bm,
             for k in range(C_TILES):
                 nc.tensor.matmul(
                     s_ps[:],
-                    lhsT=live["qT", i][:, k, :],
-                    rhs=kT[:, k, h * BANK : (h + 1) * BANK],
+                    lhsT=live["qT", i][:, :, k],
+                    rhs=kT[:, k // 2, k % 2, h * BANK : (h + 1) * BANK],
                     start=(k == 0),
                     stop=(k == C_TILES - 1),
                 )
@@ -240,7 +243,7 @@ def tile_epipolarcrossattention_pa_t_kernel(tc, Q, K, V, kpts_L, kpts_R, Wm, bm,
             for g in range(KEY_PASSES):
                 for u in range(2):
                     nc.tensor.transpose(
-                        et_ps[:, g, u, :], e_words[:, g * 2 * P + u : (g + 1) * 2 * P : 2], ident_f32[:]
+                        et_ps[:, g, u, :], e_words[:, (2 * g + u) * P : (2 * g + u + 1) * P], ident_f32[:]
                     )
             live["et_ps", i] = et_ps
 
@@ -281,17 +284,27 @@ def tile_epipolarcrossattention_pa_t_kernel(tc, Q, K, V, kpts_L, kpts_R, Wm, bm,
             )
             live["matched", i] = matched
 
-        def transpose_matched(i):
+        def transpose_matched(i, t_ps):
             m_words = live["matched", i][:].bitcast(F32)
-            mt_ps = psum.tile([P, 2, P], F32, name="mt_ps", tag="tm")
             for u in range(2):
-                nc.tensor.transpose(mt_ps[:, u, :], m_words[:, u : C // 2 : 2], ident_f32[:])
-            live["mt_ps", i] = mt_ps
+                nc.tensor.transpose(t_ps[:, 1, u, :], m_words[:, u * P : (u + 1) * P], ident_f32[:])
 
-        def copy_matched(i):
-            m_grouped = work.tile([P, P, PACK], BF16, name="m_grouped", tag="m_grouped", align_bytes=64)
-            nc.scalar.copy(out=m_grouped[:].bitcast(F32), in_=live["mt_ps", i][:].rearrange("p u n -> p n u"))
-            live["m_grouped", i] = m_grouped
+        def transpose_pair(i_q, i_m):
+            t_ps = psum.tile([P, 2, 2, P], F32, name="t_ps", tag="tqm")
+            if 0 <= i_m < TILES:
+                transpose_matched(i_m, t_ps)
+            if 0 <= i_q < TILES:
+                transpose_queries(i_q, t_ps)
+            live["t_ps", i_q] = t_ps
+
+        def copy_pair(i_q, i_m):
+            grouped = work.tile([P, 2, P, PACK], BF16, name="grouped", tag="grouped", align_bytes=64)
+            parts = slice(0 if 0 <= i_q < TILES else 1, 2 if 0 <= i_m < TILES else 1)
+            nc.scalar.copy(
+                out=grouped[:].bitcast(F32)[:, parts], in_=live["t_ps", i_q][:].rearrange("p k u n -> p k n u")[:, parts]
+            )
+            live["qT", i_q] = grouped[:, 0]
+            live["m_grouped", i_m] = grouped[:, 1]
 
         def quantise_matched(i):
             m_codes = work.tile([P, P], U32, name="m_codes", tag="m_codes", align_bytes=64)
@@ -299,13 +312,13 @@ def tile_epipolarcrossattention_pa_t_kernel(tc, Q, K, V, kpts_L, kpts_R, Wm, bm,
             nc.vector.quantize_mx(
                 out=m_codes[:].bitcast(FP8X4),
                 scales=m_scales[:],
-                in_=live["m_grouped", i][:].rearrange("p n t -> p (n t)"),
+                in_=live["m_grouped", i].rearrange("p n t -> p (n t)"),
             )
             live["m_codes", i] = m_codes
             live["m_scales", i] = m_scales
 
         def project(i):
-            o_ps = psum.tile([P, C], F32, name="o_ps", tag="fo")
+            o_ps = psum.tile([P, C], F32, name="o_ps", tag="fo", bufs=2)
             nc.tensor.matmul_mx(
                 out=o_ps[:],
                 lhsT=live["m_codes", i][:].bitcast(FP8X4),
@@ -326,36 +339,44 @@ def tile_epipolarcrossattention_pa_t_kernel(tc, Q, K, V, kpts_L, kpts_R, Wm, bm,
             if 0 <= i < TILES:
                 stage(i, *args)
 
+        def on_pair(stage, i_q, i_m):
+            if 0 <= i_q < TILES or 0 <= i_m < TILES:
+                stage(i_q, i_m)
+
         def step(k):
             on_tile(transpose_e, k - 2)
-            on_tile(transpose_matched, k - 5)
-            on_tile(transpose_queries, k + 2)
+            on_pair(transpose_pair, k + 2, k - 5)
             on_tile(exponentials, k - 1)
             on_tile(normalise, k - 4)
             on_tile(mask_scores, k, 1)
-            on_tile(join_mask, k + 1)
-            on_tile(add_bias_and_store, k - 7)
             on_tile(quantise_matched, k - 6)
+            on_tile(join_mask, k + 1)
+            on_tile(add_bias_and_store, k - 8)
             on_tile(row_minimum, k)
+            on_tile(mask_offset_v, k + 3)
             on_tile(exp_bias, k)
             on_tile(copy_e, k - 2)
-            on_tile(copy_matched, k - 5)
-            on_tile(copy_queries, k + 2)
+            on_pair(copy_pair, k + 2, k - 5)
             on_tile(scores, k + 1, 0)
             on_tile(invert_sum, k - 2)
-            on_tile(mask_offset_v, k + 2)
-            on_tile(quantise_e, k - 2)
             on_tile(mask_distance_u, k + 3)
             on_tile(weighted_sum, k - 3)
-            on_tile(project, k - 6)
+            on_tile(project, k - 7)
             on_tile(mask_scores, k + 1, 0)
+            on_tile(quantise_e, k - 2)
             on_tile(scores, k + 1, 1)
 
         step(-3)
         step(-2)
         step(-1)
+        group_values(0, 0)
         step(0)
-        quantise_values()
         quantise_weights()
-        for k in range(1, TILES + 7):
+        group_values(0, 1)
+        step(1)
+        group_values(1, 0)
+        group_values(1, 1)
+        step(2)
+        quantise_values()
+        for k in range(3, TILES + 8):
             step(k)

@@ -41,41 +41,44 @@ def tile_epipolarcrossattention_pa_t_kernel(tc, Q, K, V, kpts_L, kpts_R, Wm, bm,
         work = ctx.enter_context(tc.tile_pool(name="work", bufs=3))
         psum = ctx.enter_context(tc.psum_pool(name="psum", bufs=1))
 
-        ident_f32 = const.tile([P, P], F32, name="ident_f32")
-        make_identity(nc, ident_f32[:])
-
         query_uv = const.tile([P, TILES, 2], BF16, name="query_uv")
         nc.scalar.dma_start(out=query_uv[:], in_=kpts_L.rearrange("(p i) t -> p i t", i=TILES))
-        key_uv = const.tile([P, KEYS, 2], BF16, name="key_uv")
-        nc.scalar.dma_start(
-            out=key_uv[:].rearrange("p m t -> p (m t)"),
-            in_=kpts_R.rearrange("m t -> (m t)").partition_broadcast(P),
-        )
         k_rows = const.tile([P, KEY_TILES, C], BF16, name="k_rows")
         k_view = K.rearrange("(j p) c -> p j c", p=P)
         nc.sync.dma_start(out=k_rows[:, 0:4, :], in_=k_view[:, 0:4, :])
-        nc.sync.dma_start(out=k_rows[:, 4:8, :], in_=k_view[:, 4:8, :])
         q_rows = const.tile([P, TILES, C], BF16, name="q_rows")
         q_view = Q.rearrange("(p i) c -> p i c", i=TILES)
         nc.sync.dma_start(out=q_rows[:, 0:2, :], in_=q_view[:, 0:2, :])
+        nc.sync.dma_start(out=k_rows[:, 4:8, :], in_=k_view[:, 4:8, :])
+        key_uv = const.tile([P, KEYS, 2], BF16, name="key_uv")
+        nc.sync.dma_start(
+            out=key_uv[:].rearrange("p m t -> p (m t)"),
+            in_=kpts_R.rearrange("m t -> (m t)").partition_broadcast(P),
+        )
         v_rows = const.tile([P, KEY_PASSES, PACK, C], BF16, name="v_rows")
         for g in range(KEY_PASSES):
             nc.sync.dma_start(
                 out=v_rows[:, g].rearrange("p (u e) c -> p u (e c)", e=2),
                 in_=V[g * P * PACK : (g + 1) * P * PACK, :].rearrange("(u p e) c -> p u (e c)", u=2, e=2),
             )
-        nc.sync.dma_start(out=q_rows[:, 2:4, :], in_=q_view[:, 2:4, :])
         w_rows = const.tile([P, C_TILES, C], BF16, name="w_rows")
         nc.sync.dma_start(out=w_rows[:], in_=Wm.rearrange("(a p) c -> p a c", p=P))
+        nc.sync.dma_start(out=q_rows[:, 2:4, :], in_=q_view[:, 2:4, :])
         bias_row = const.tile([P, C], BF16, name="bias_row")
         nc.sync.dma_start(out=bias_row[:], in_=bm.partition_broadcast(P))
         for first in range(4, TILES, 4):
             nc.sync.dma_start(out=q_rows[:, first : first + 4, :], in_=q_view[:, first : first + 4, :])
 
+        ident_f32 = const.tile([P, P], F32, name="ident_f32")
+        make_identity(nc, ident_f32[:])
+
+        no_value = const.tile([P, 1], F32, name="no_value")
+        nc.vector.memset(no_value[:], 0.0)
+        table_loaded = const.tile([P, 1], F32, name="table_loaded")
+        nc.scalar.activation(out=table_loaded[:], in_=no_value[:], func=ACT.Exp)
+
         bias_v = const.tile([P, TILES], F32, name="bias_v")
         nc.vector.tensor_scalar(out=bias_v[:], in0=query_uv[:, :, 1], scalar1=-1.0, scalar2=None, op0=ALU.mult)
-        key_v = const.tile([P, KEYS], BF16, name="key_v")
-        nc.vector.tensor_copy(out=key_v[:], in_=key_uv[:, :, 1])
         bias_u = const.tile([P, TILES], F32, name="bias_u")
         nc.vector.tensor_scalar(
             out=bias_u[:], in0=query_uv[:, :, 0], scalar1=U_HALF, scalar2=-U_STRETCH, op0=ALU.subtract, op1=ALU.mult
@@ -83,17 +86,19 @@ def tile_epipolarcrossattention_pa_t_kernel(tc, Q, K, V, kpts_L, kpts_R, Wm, bm,
 
         kT = const.tile([P, 2, 2, KEYS], BF16, name="kT")
         k_words = k_rows[:].bitcast(F32)
-        for j in range(KEY_TILES):
+
+        def transpose_keys(j, copied_by_vector):
             kt_ps = psum.tile([P, 2, P], F32, name="kt_ps", tag="scores", bufs=3)
             for u in range(2):
                 nc.tensor.transpose(kt_ps[:, u, :], k_words[:, j, u * P : (u + 1) * P], ident_f32[:])
-            nc.vector.tensor_scalar(
-                out=kT[:, :, :, j * P : (j + 1) * P],
-                in0=kt_ps[:].bitcast(BF16).rearrange("p u (m e) -> p u e m", e=2),
-                scalar1=TINY,
-                scalar2=None,
-                op0=ALU.mult,
-            )
+            kt_out = kT[:, :, :, j * P : (j + 1) * P]
+            kt_in = kt_ps[:].bitcast(BF16).rearrange("p u (m e) -> p u e m", e=2)
+            if copied_by_vector:
+                nc.vector.tensor_scalar(out=kt_out, in0=kt_in, scalar1=TINY, scalar2=None, op0=ALU.mult)
+            else:
+                nc.scalar.activation(out=kt_out, in_=kt_in, func=ACT.Copy, scale=TINY)
+
+        key_v = const.tile([P, KEYS], BF16, name="key_v")
 
         v_codes = const.tile([P, KEY_PASSES, C], U32, name="v_codes", align_bytes=64)
         v_scales = const.tile([P, KEY_PASSES, C], U8, name="v_scales", align_bytes=64)
@@ -122,17 +127,21 @@ def tile_epipolarcrossattention_pa_t_kernel(tc, Q, K, V, kpts_L, kpts_R, Wm, bm,
         w_codes = const.tile([P, C], U32, name="w_codes", align_bytes=64)
         w_scales = const.tile([P, C], U8, name="w_scales", align_bytes=64)
 
+        w_grouped = const.tile([P, C, PACK], BF16, name="w_grouped", align_bytes=64)
+        w_words = w_rows[:].bitcast(F32)
+
+        def transpose_weights(a):
+            wt_ps = psum.tile([P, 2, P], F32, name="wt_ps", tag="fo", bufs=2)
+            for u in range(2):
+                nc.tensor.transpose(wt_ps[:, u, :], w_words[:, a, u * P : (u + 1) * P], ident_f32[:])
+            w_out = w_grouped[:].bitcast(F32)[:, a * P : (a + 1) * P, :]
+            w_in = wt_ps[:].rearrange("p u o -> p o u")
+            if a % 2:
+                nc.vector.tensor_copy(out=w_out, in_=w_in)
+            else:
+                nc.scalar.copy(out=w_out, in_=w_in)
+
         def quantise_weights():
-            w_grouped = const.tile([P, C, PACK], BF16, name="w_grouped", align_bytes=64)
-            w_words = w_rows[:].bitcast(F32)
-            for a in range(C_TILES):
-                wt_ps = psum.tile([P, 2, P], F32, name="wt_ps", tag="fo", bufs=2)
-                for u in range(2):
-                    nc.tensor.transpose(wt_ps[:, u, :], w_words[:, a, u * P : (u + 1) * P], ident_f32[:])
-                nc.scalar.copy(
-                    out=w_grouped[:].bitcast(F32)[:, a * P : (a + 1) * P, :],
-                    in_=wt_ps[:].rearrange("p u o -> p o u"),
-                )
             nc.vector.quantize_mx(
                 out=w_codes[:].bitcast(FP8X4), scales=w_scales[:], in_=w_grouped[:].rearrange("p o t -> p (o t)")
             )
@@ -147,7 +156,8 @@ def tile_epipolarcrossattention_pa_t_kernel(tc, Q, K, V, kpts_L, kpts_R, Wm, bm,
 
         def mask_offset_v(i):
             off_v = work.tile([P, KEYS], BF16, name="off_v", tag="off_v", bufs=2)
-            nc.gpsimd.tensor_scalar(
+            engine = nc.vector if i < 2 else nc.gpsimd
+            engine.tensor_scalar(
                 out=off_v[:],
                 in0=key_v[:],
                 scalar1=bias_v[:, i : i + 1],
@@ -290,7 +300,8 @@ def tile_epipolarcrossattention_pa_t_kernel(tc, Q, K, V, kpts_L, kpts_R, Wm, bm,
                 nc.tensor.transpose(t_ps[:, 1, u, :], m_words[:, u * P : (u + 1) * P], ident_f32[:])
 
         def transpose_pair(i_q, i_m):
-            t_ps = psum.tile([P, 2, 2, P], F32, name="t_ps", tag="tqm")
+            tag, bufs = ("tqm", 1) if i_q < TILES else ("scores", 3)
+            t_ps = psum.tile([P, 2, 2, P], F32, name="t_ps", tag=tag, bufs=bufs)
             if 0 <= i_m < TILES:
                 transpose_matched(i_m, t_ps)
             if 0 <= i_q < TILES:
@@ -346,8 +357,10 @@ def tile_epipolarcrossattention_pa_t_kernel(tc, Q, K, V, kpts_L, kpts_R, Wm, bm,
         def step(k):
             on_tile(transpose_e, k - 2)
             on_pair(transpose_pair, k + 2, k - 5)
-            on_tile(exponentials, k - 1)
             on_tile(normalise, k - 4)
+            on_tile(copy_e, k - 2)
+            on_pair(copy_pair, k + 2, k - 5)
+            on_tile(exponentials, k - 1)
             on_tile(mask_scores, k, 1)
             on_tile(quantise_matched, k - 6)
             on_tile(join_mask, k + 1)
@@ -355,8 +368,6 @@ def tile_epipolarcrossattention_pa_t_kernel(tc, Q, K, V, kpts_L, kpts_R, Wm, bm,
             on_tile(row_minimum, k)
             on_tile(mask_offset_v, k + 3)
             on_tile(exp_bias, k)
-            on_tile(copy_e, k - 2)
-            on_pair(copy_pair, k + 2, k - 5)
             on_tile(scores, k + 1, 0)
             on_tile(invert_sum, k - 2)
             on_tile(mask_distance_u, k + 3)
@@ -366,17 +377,32 @@ def tile_epipolarcrossattention_pa_t_kernel(tc, Q, K, V, kpts_L, kpts_R, Wm, bm,
             on_tile(quantise_e, k - 2)
             on_tile(scores, k + 1, 1)
 
-        step(-3)
-        step(-2)
-        step(-1)
+        for j in range(4):
+            transpose_keys(j, copied_by_vector=j % 2 == 0)
+        transpose_pair(0, -1)
+        copy_pair(0, -1)
+        transpose_keys(4, copied_by_vector=True)
+        transpose_keys(5, copied_by_vector=False)
+        transpose_keys(6, copied_by_vector=True)
+        nc.vector.tensor_copy(out=key_v[:], in_=key_uv[:, :, 1])
+        mask_offset_v(0)
+        mask_distance_u(0)
+        transpose_keys(7, copied_by_vector=True)
+        mask_offset_v(1)
+        mask_distance_u(1)
         group_values(0, 0)
-        step(0)
-        quantise_weights()
         group_values(0, 1)
-        step(1)
+        step(-1)
+        transpose_weights(0)
+        transpose_weights(1)
         group_values(1, 0)
+        step(0)
+        transpose_weights(2)
+        transpose_weights(3)
         group_values(1, 1)
+        step(1)
         step(2)
         quantise_values()
+        quantise_weights()
         for k in range(3, TILES + 8):
             step(k)

@@ -41,6 +41,10 @@ def tile_epipolarcrossattention_pa_t_kernel(tc, Q, K, V, kpts_L, kpts_R, Wm, bm,
         work = ctx.enter_context(tc.tile_pool(name="work", bufs=3))
         psum = ctx.enter_context(tc.psum_pool(name="psum", bufs=1))
 
+        key_line = const.tile([P, 2 * KEYS], BF16, name="key_line")
+        nc.vector.memset(key_line[:, 0:KEYS].bitcast(I32), 0)
+        nc.gpsimd.memset(key_line[:, KEYS:].bitcast(I32), 0)
+        nc.scalar.dma_start(out=key_line[0:1, :], in_=kpts_R.rearrange("(a m) t -> a (m t)", a=1))
         query_uv = const.tile([P, TILES, 2], BF16, name="query_uv")
         nc.scalar.dma_start(out=query_uv[:], in_=kpts_L.rearrange("(p i) t -> p i t", i=TILES))
         k_rows = const.tile([P, KEY_TILES, C], BF16, name="k_rows")
@@ -50,11 +54,6 @@ def tile_epipolarcrossattention_pa_t_kernel(tc, Q, K, V, kpts_L, kpts_R, Wm, bm,
         q_view = Q.rearrange("(p i) c -> p i c", i=TILES)
         nc.sync.dma_start(out=q_rows[:, 0:2, :], in_=q_view[:, 0:2, :])
         nc.sync.dma_start(out=k_rows[:, 4:8, :], in_=k_view[:, 4:8, :])
-        key_uv = const.tile([P, KEYS, 2], BF16, name="key_uv")
-        nc.sync.dma_start(
-            out=key_uv[:].rearrange("p m t -> p (m t)"),
-            in_=kpts_R.rearrange("m t -> (m t)").partition_broadcast(P),
-        )
         v_rows = const.tile([P, KEY_PASSES, PACK, C], BF16, name="v_rows")
         for g in range(KEY_PASSES):
             nc.sync.dma_start(
@@ -72,6 +71,9 @@ def tile_epipolarcrossattention_pa_t_kernel(tc, Q, K, V, kpts_L, kpts_R, Wm, bm,
         ident_f32 = const.tile([P, P], F32, name="ident_f32")
         make_identity(nc, ident_f32[:])
 
+        ones = const.tile([P, P], BF16, name="ones")
+        nc.vector.memset(ones[:], 1.0)
+
         no_value = const.tile([P, 1], F32, name="no_value")
         nc.vector.memset(no_value[:], 0.0)
         table_loaded = const.tile([P, 1], F32, name="table_loaded")
@@ -84,21 +86,35 @@ def tile_epipolarcrossattention_pa_t_kernel(tc, Q, K, V, kpts_L, kpts_R, Wm, bm,
             out=bias_u[:], in0=query_uv[:, :, 0], scalar1=U_HALF, scalar2=-U_STRETCH, op0=ALU.subtract, op1=ALU.mult
         )
 
-        kT = const.tile([P, 2, 2, KEYS], BF16, name="kT")
-        k_words = k_rows[:].bitcast(F32)
+        kT = const.tile([P, C_TILES, KEYS], BF16, name="kT")
+        ident_bf = const.tile([P, P], BF16, name="ident_bf")
+        nc.vector.tensor_copy(out=ident_bf[:], in_=ident_f32[:])
 
-        def transpose_keys(j, copied_by_vector):
-            kt_ps = psum.tile([P, 2, P], F32, name="kt_ps", tag="scores", bufs=3)
+        def transpose_keys(j, tag, bufs):
+            kt_ps = psum.tile([P, C_TILES, P], BF16, name="kt_ps", tag=tag, bufs=bufs)
             for u in range(2):
-                nc.tensor.transpose(kt_ps[:, u, :], k_words[:, j, u * P : (u + 1) * P], ident_f32[:])
-            kt_out = kT[:, :, :, j * P : (j + 1) * P]
-            kt_in = kt_ps[:].bitcast(BF16).rearrange("p u (m e) -> p u e m", e=2)
-            if copied_by_vector:
-                nc.vector.tensor_scalar(out=kt_out, in0=kt_in, scalar1=TINY, scalar2=None, op0=ALU.mult)
-            else:
-                nc.scalar.activation(out=kt_out, in_=kt_in, func=ACT.Copy, scale=TINY)
+                for e in range(2):
+                    nc.tensor.transpose(
+                        kt_ps[:, 2 * u + e, :], k_rows[:, j, 2 * P * u + e : 2 * P * (u + 1) : 2], ident_bf[:]
+                    )
+            nc.vector.tensor_scalar(
+                out=kT[:, :, j * P : (j + 1) * P], in0=kt_ps[:], scalar1=TINY, scalar2=None, op0=ALU.mult
+            )
 
-        key_v = const.tile([P, KEYS], BF16, name="key_v")
+        key_tm = const.tile([P, 2, KEYS], BF16, name="key_tm")
+
+        def broadcast_keys(j, tag, bufs, copied_by_vector):
+            b_ps = psum.tile([P, BANK], F32, name="b_ps", tag=tag, bufs=bufs)
+            nc.tensor.matmul(
+                b_ps[:], lhsT=ones[:], rhs=key_line[:, j * BANK : (j + 1) * BANK], start=True, stop=True
+            )
+            b_out = key_tm[:, :, j * BANK // 2 : (j + 1) * BANK // 2]
+            b_in = b_ps[:].rearrange("p (m t) -> p t m", t=2)
+            if copied_by_vector:
+                nc.vector.tensor_copy(out=b_out, in_=b_in)
+            else:
+                nc.scalar.copy(out=b_out, in_=b_in)
+
 
         v_codes = const.tile([P, KEY_PASSES, C], U32, name="v_codes", align_bytes=64)
         v_scales = const.tile([P, KEY_PASSES, C], U8, name="v_scales", align_bytes=64)
@@ -136,10 +152,7 @@ def tile_epipolarcrossattention_pa_t_kernel(tc, Q, K, V, kpts_L, kpts_R, Wm, bm,
                 nc.tensor.transpose(wt_ps[:, u, :], w_words[:, a, u * P : (u + 1) * P], ident_f32[:])
             w_out = w_grouped[:].bitcast(F32)[:, a * P : (a + 1) * P, :]
             w_in = wt_ps[:].rearrange("p u o -> p o u")
-            if a % 2:
-                nc.vector.tensor_copy(out=w_out, in_=w_in)
-            else:
-                nc.scalar.copy(out=w_out, in_=w_in)
+            nc.scalar.copy(out=w_out, in_=w_in)
 
         def quantise_weights():
             nc.vector.quantize_mx(
@@ -159,7 +172,7 @@ def tile_epipolarcrossattention_pa_t_kernel(tc, Q, K, V, kpts_L, kpts_R, Wm, bm,
             engine = nc.vector if i < 2 else nc.gpsimd
             engine.tensor_scalar(
                 out=off_v[:],
-                in0=key_v[:],
+                in0=key_tm[:, 1, :],
                 scalar1=bias_v[:, i : i + 1],
                 scalar2=V_STRETCH,
                 op0=ALU.add,
@@ -170,7 +183,7 @@ def tile_epipolarcrossattention_pa_t_kernel(tc, Q, K, V, kpts_L, kpts_R, Wm, bm,
         def mask_distance_u(i):
             far_u = work.tile([P, KEYS], BF16, name="far_u", tag="far_u")
             nc.scalar.activation(
-                out=far_u[:], in_=key_uv[:, :, 0], func=ACT.Abs, scale=U_STRETCH, bias=bias_u[:, i : i + 1]
+                out=far_u[:], in_=key_tm[:, 0, :], func=ACT.Abs, scale=U_STRETCH, bias=bias_u[:, i : i + 1]
             )
             live["far_u", i] = far_u
 
@@ -192,7 +205,7 @@ def tile_epipolarcrossattention_pa_t_kernel(tc, Q, K, V, kpts_L, kpts_R, Wm, bm,
                 nc.tensor.matmul(
                     s_ps[:],
                     lhsT=live["qT", i][:, :, k],
-                    rhs=kT[:, k // 2, k % 2, h * BANK : (h + 1) * BANK],
+                    rhs=kT[:, k, h * BANK : (h + 1) * BANK],
                     start=(k == 0),
                     stop=(k == C_TILES - 1),
                 )
@@ -364,7 +377,7 @@ def tile_epipolarcrossattention_pa_t_kernel(tc, Q, K, V, kpts_L, kpts_R, Wm, bm,
             on_tile(mask_scores, k, 1)
             on_tile(quantise_matched, k - 6)
             on_tile(join_mask, k + 1)
-            on_tile(add_bias_and_store, k - 8)
+            on_tile(add_bias_and_store, k - 7)
             on_tile(row_minimum, k)
             on_tile(mask_offset_v, k + 3)
             on_tile(exp_bias, k)
@@ -372,24 +385,23 @@ def tile_epipolarcrossattention_pa_t_kernel(tc, Q, K, V, kpts_L, kpts_R, Wm, bm,
             on_tile(invert_sum, k - 2)
             on_tile(mask_distance_u, k + 3)
             on_tile(weighted_sum, k - 3)
-            on_tile(project, k - 7)
+            on_tile(project, k - 6)
             on_tile(mask_scores, k + 1, 0)
             on_tile(quantise_e, k - 2)
             on_tile(scores, k + 1, 1)
 
+        for j, (tag, bufs) in enumerate((("fo", 2), ("fo", 2), ("te", 1), ("pv", 1))):
+            broadcast_keys(j, tag, bufs, copied_by_vector=j < 1)
+        mask_distance_u(0)
         for j in range(4):
-            transpose_keys(j, copied_by_vector=j % 2 == 0)
+            transpose_keys(j, "scores", 3)
         transpose_pair(0, -1)
         copy_pair(0, -1)
-        transpose_keys(4, copied_by_vector=True)
-        transpose_keys(5, copied_by_vector=False)
-        transpose_keys(6, copied_by_vector=True)
-        nc.vector.tensor_copy(out=key_v[:], in_=key_uv[:, :, 1])
-        mask_offset_v(0)
-        mask_distance_u(0)
-        transpose_keys(7, copied_by_vector=True)
-        mask_offset_v(1)
         mask_distance_u(1)
+        for j in range(4, KEY_TILES):
+            transpose_keys(j, "fo", 2)
+        mask_offset_v(0)
+        mask_offset_v(1)
         group_values(0, 0)
         group_values(0, 1)
         step(-1)
@@ -404,5 +416,5 @@ def tile_epipolarcrossattention_pa_t_kernel(tc, Q, K, V, kpts_L, kpts_R, Wm, bm,
         step(2)
         quantise_values()
         quantise_weights()
-        for k in range(3, TILES + 8):
+        for k in range(3, TILES + 7):
             step(k)

import math
from contextlib import ExitStack

import concourse.mybir as mybir
from concourse.masks import make_identity

BF16 = mybir.dt.bfloat16
F32 = mybir.dt.float32
U32 = mybir.dt.uint32
U8 = mybir.dt.uint8
I32 = mybir.dt.int32
FP8X4 = mybir.dt.float8_e4m3fn_x4
ALU = mybir.AluOpType
ACT = mybir.ActivationFunctionType

P = 128
PACK = 4
QUERIES, KEYS, C = 4096, 1024, 512
TILES = QUERIES // P
KEY_TILES = KEYS // P
C_TILES = C // P
BANK = 512
KEY_PASSES = KEYS // (P * PACK)

FLOPS = 2 * QUERIES * KEYS * C * 2 + 2 * QUERIES * C * C

FAR = 512.0
U_HALF = 96.0
V_STRETCH = 192.0
U_STRETCH = 5.375

TINY = 2.0**-80
E_SCALE = 1.0 / (TINY * math.sqrt(C))


def tile_epipolarcrossattention_pa_t_kernel(tc, Q, K, V, kpts_L, kpts_R, Wm, bm, out):
    nc = tc.nc
    with ExitStack() as ctx:
        ctx.enter_context(tc.manual_schedule())
        const = ctx.enter_context(tc.tile_pool(name="const", bufs=1))
        work = ctx.enter_context(tc.tile_pool(name="work", bufs=3))
        psum = ctx.enter_context(tc.psum_pool(name="psum", bufs=1))

        key_line = const.tile([P, 2 * KEYS], BF16, name="key_line")
        nc.vector.memset(key_line[:, 0:KEYS].bitcast(I32), 0)
        nc.gpsimd.memset(key_line[:, KEYS:].bitcast(I32), 0)
        nc.scalar.dma_start(out=key_line[0:1, :], in_=kpts_R.rearrange("(a m) t -> a (m t)", a=1))
        query_uv = const.tile([P, TILES, 2], BF16, name="query_uv")
        nc.scalar.dma_start(out=query_uv[:], in_=kpts_L.rearrange("(p i) t -> p i t", i=TILES))
        k_rows = const.tile([P, KEY_TILES, C], BF16, name="k_rows")
        k_view = K.rearrange("(j p) c -> p j c", p=P)
        nc.sync.dma_start(out=k_rows[:, 0:4, :], in_=k_view[:, 0:4, :])
        q_rows = const.tile([P, TILES, C], BF16, name="q_rows")
        q_view = Q.rearrange("(p i) c -> p i c", i=TILES)
        nc.sync.dma_start(out=q_rows[:, 0:2, :], in_=q_view[:, 0:2, :])
        nc.sync.dma_start(out=k_rows[:, 4:8, :], in_=k_view[:, 4:8, :])
        v_rows = const.tile([P, KEY_PASSES, PACK, C], BF16, name="v_rows")
        for g in range(KEY_PASSES):
            nc.sync.dma_start(
                out=v_rows[:, g].rearrange("p (u e) c -> p u (e c)", e=2),
                in_=V[g * P * PACK : (g + 1) * P * PACK, :].rearrange("(u p e) c -> p u (e c)", u=2, e=2),
            )
        w_rows = const.tile([P, C_TILES, C], BF16, name="w_rows")
        nc.sync.dma_start(out=w_rows[:], in_=Wm.rearrange("(a p) c -> p a c", p=P))
        nc.sync.dma_start(out=q_rows[:, 2:4, :], in_=q_view[:, 2:4, :])
        bias_row = const.tile([P, C], BF16, name="bias_row")
        nc.sync.dma_start(out=bias_row[:], in_=bm.partition_broadcast(P))
        for first in range(4, TILES, 4):
            nc.sync.dma_start(out=q_rows[:, first : first + 4, :], in_=q_view[:, first : first + 4, :])

        ident_f32 = const.tile([P, P], F32, name="ident_f32")
        make_identity(nc, ident_f32[:])

        ones = const.tile([P, P], BF16, name="ones")
        nc.vector.memset(ones[:], 1.0)

        no_value = const.tile([P, 1], F32, name="no_value")
        nc.vector.memset(no_value[:], 0.0)
        table_loaded = const.tile([P, 1], F32, name="table_loaded")
        nc.scalar.activation(out=table_loaded[:], in_=no_value[:], func=ACT.Exp)

        bias_v = const.tile([P, TILES], F32, name="bias_v")
        nc.vector.tensor_scalar(out=bias_v[:], in0=query_uv[:, :, 1], scalar1=-1.0, scalar2=None, op0=ALU.mult)
        bias_u = const.tile([P, TILES], F32, name="bias_u")
        nc.vector.tensor_scalar(
            out=bias_u[:], in0=query_uv[:, :, 0], scalar1=U_HALF, scalar2=-U_STRETCH, op0=ALU.subtract, op1=ALU.mult
        )

        kT = const.tile([P, C_TILES, KEYS], BF16, name="kT")
        ident_bf = const.tile([P, P], BF16, name="ident_bf")
        nc.vector.tensor_copy(out=ident_bf[:], in_=ident_f32[:])

        def transpose_keys(j, tag, bufs):
            kt_ps = psum.tile([P, C_TILES, P], BF16, name="kt_ps", tag=tag, bufs=bufs)
            for u in range(2):
                for e in range(2):
                    nc.tensor.transpose(
                        kt_ps[:, 2 * u + e, :], k_rows[:, j, 2 * P * u + e : 2 * P * (u + 1) : 2], ident_bf[:]
                    )
            nc.vector.tensor_scalar(
                out=kT[:, :, j * P : (j + 1) * P], in0=kt_ps[:], scalar1=TINY, scalar2=None, op0=ALU.mult
            )

        key_tm = const.tile([P, 2, KEYS], BF16, name="key_tm")

        def broadcast_keys(j, tag, bufs, copied_by_vector):
            b_ps = psum.tile([P, BANK], F32, name="b_ps", tag=tag, bufs=bufs)
            nc.tensor.matmul(
                b_ps[:], lhsT=ones[:], rhs=key_line[:, j * BANK : (j + 1) * BANK], start=True, stop=True
            )
            b_out = key_tm[:, :, j * BANK // 2 : (j + 1) * BANK // 2]
            b_in = b_ps[:].rearrange("p (m t) -> p t m", t=2)
            if copied_by_vector:
                nc.vector.tensor_copy(out=b_out, in_=b_in)
            else:
                nc.scalar.copy(out=b_out, in_=b_in)


        v_codes = const.tile([P, KEY_PASSES, C], U32, name="v_codes", align_bytes=64)
        v_scales = const.tile([P, KEY_PASSES, C], U8, name="v_scales", align_bytes=64)

        v_grouped = const.tile([P, KEY_PASSES, C, PACK], BF16, name="v_grouped", align_bytes=64)

        def group_values(g, half):
            cols = slice(half * C // 2, (half + 1) * C // 2)
            nc.gpsimd.tensor_scalar(
                out=v_grouped[:, g, cols, :],
                in0=v_rows[:, g, :, cols].rearrange("p t c -> p c t"),
                scalar1=1.0,
                scalar2=0.0,
                op0=ALU.mult,
                op1=ALU.add,
            )

        def quantise_values():
            for g in range(KEY_PASSES):
                nc.vector.quantize_mx(
                    out=v_codes[:, g, :].bitcast(FP8X4),
                    scales=v_scales[:, g, :],
                    in_=v_grouped[:, g].rearrange("p c t -> p (c t)"),
                )

        w_codes = const.tile([P, C], U32, name="w_codes", align_bytes=64)
        w_scales = const.tile([P, C], U8, name="w_scales", align_bytes=64)

        w_grouped = const.tile([P, C, PACK], BF16, name="w_grouped", align_bytes=64)
        w_words = w_rows[:].bitcast(F32)

        def transpose_weights(a):
            wt_ps = psum.tile([P, 2, P], F32, name="wt_ps", tag="fo", bufs=2)
            for u in range(2):
                nc.tensor.transpose(wt_ps[:, u, :], w_words[:, a, u * P : (u + 1) * P], ident_f32[:])
            w_out = w_grouped[:].bitcast(F32)[:, a * P : (a + 1) * P, :]
            w_in = wt_ps[:].rearrange("p u o -> p o u")
            nc.scalar.copy(out=w_out, in_=w_in)

        def quantise_weights():
            nc.vector.quantize_mx(
                out=w_codes[:].bitcast(FP8X4), scales=w_scales[:], in_=w_grouped[:].rearrange("p o t -> p (o t)")
            )

        out_view = out.rearrange("(p i) o -> p i o", i=TILES)
        live = {}

        def transpose_queries(i, t_ps):
            q_words = q_rows[:].bitcast(F32)
            for u in range(2):
                nc.tensor.transpose(t_ps[:, 0, u, :], q_words[:, i, u * P : (u + 1) * P], ident_f32[:])

        def mask_offset_v(i):
            off_v = work.tile([P, KEYS], BF16, name="off_v", tag="off_v", bufs=2)
            engine = nc.vector if i < 2 else nc.gpsimd
            engine.tensor_scalar(
                out=off_v[:],
                in0=key_tm[:, 1, :],
                scalar1=bias_v[:, i : i + 1],
                scalar2=V_STRETCH,
                op0=ALU.add,
                op1=ALU.mult,
            )
            live["off_v", i] = off_v

        def mask_distance_u(i):
            far_u = work.tile([P, KEYS], BF16, name="far_u", tag="far_u")
            nc.scalar.activation(
                out=far_u[:], in_=key_tm[:, 0, :], func=ACT.Abs, scale=U_STRETCH, bias=bias_u[:, i : i + 1]
            )
            live["far_u", i] = far_u

        def join_mask(i):
            far = work.tile([P, KEYS], BF16, name="far", tag="far")
            nc.vector.scalar_tensor_tensor(
                out=far[:].bitcast(I32),
                in0=live["off_v", i][:].bitcast(I32),
                scalar=0x7FFF7FFF,
                in1=live["far_u", i][:].bitcast(I32),
                op0=ALU.bitwise_and,
                op1=ALU.bitwise_or,
            )
            live["far", i] = far

        def scores(i, h):
            s_ps = psum.tile([P, BANK], F32, name="s_ps", tag="scores", bufs=3)
            for k in range(C_TILES):
                nc.tensor.matmul(
                    s_ps[:],
                    lhsT=live["qT", i][:, :, k],
                    rhs=kT[:, k, h * BANK : (h + 1) * BANK],
                    start=(k == 0),
                    stop=(k == C_TILES - 1),
                )
            live["s_ps", i, h] = s_ps

        def mask_scores(i, h):
            if h == 0:
                live["neg", i] = work.tile([P, KEYS], F32, name="neg", tag="neg", bufs=4)
            cols = slice(h * BANK, (h + 1) * BANK)
            nc.vector.scalar_tensor_tensor(
                out=live["neg", i][:, cols],
                in0=live["far", i][:, cols],
                scalar=FAR,
                in1=live["s_ps", i, h][:],
                op0=ALU.is_ge,
                op1=ALU.subtract,
            )

        def row_minimum(i):
            low = work.tile([P, 1], F32, name="low", tag="low")
            nc.vector.tensor_reduce(out=low[:], in_=live["neg", i][:], axis=mybir.AxisListType.X, op=ALU.min)
            live["low", i] = low

        def exp_bias(i):
            e_bias = work.tile([P, 1], F32, name="e_bias", tag="e_bias")
            nc.gpsimd.tensor_scalar(
                out=e_bias[:],
                in0=live["low", i][:],
                scalar1=E_SCALE,
                scalar2=1.0,
                op0=ALU.mult,
                op1=ALU.mult,
            )
            live["e_bias", i] = e_bias

        def exponentials(i):
            e_rows = work.tile([P, KEYS], BF16, name="e_rows", tag="e_rows")
            e_sum = work.tile([P, 1], F32, name="e_sum", tag="e_sum")
            nc.scalar.activation(
                out=e_rows[:],
                in_=live["neg", i][:],
                func=ACT.Exp,
                scale=-E_SCALE,
                bias=live["e_bias", i][:, 0:1],
                accum_out=e_sum[:, 0:1],
            )
            live["e_rows", i] = e_rows
            live["e_sum", i] = e_sum

        def invert_sum(i):
            e_inv = work.tile([P, 1], F32, name="e_inv", tag="e_inv", bufs=4)
            nc.vector.reciprocal(out=e_inv[:], in_=live["e_sum", i][:])
            live["e_inv", i] = e_inv

        def transpose_e(i):
            e_words = live["e_rows", i][:].bitcast(F32)
            et_ps = psum.tile([P, KEY_PASSES, 2, P], F32, name="et_ps", tag="te")
            for g in range(KEY_PASSES):
                for u in range(2):
                    nc.tensor.transpose(
                        et_ps[:, g, u, :], e_words[:, (2 * g + u) * P : (2 * g + u + 1) * P], ident_f32[:]
                    )
            live["et_ps", i] = et_ps

        def copy_e(i):
            e_grouped = work.tile([P, KEY_PASSES, P, PACK], BF16, name="e_grouped", tag="e_grouped", align_bytes=64)
            nc.scalar.copy(out=e_grouped[:].bitcast(F32), in_=live["et_ps", i][:].rearrange("p g u n -> p g n u"))
            live["e_grouped", i] = e_grouped

        def quantise_e(i):
            e_codes = work.tile([P, KEY_PASSES, P], U32, name="e_codes", tag="e_codes", align_bytes=64)
            e_scales = work.tile([P, KEY_PASSES, P], U8, name="e_scales", tag="e_scales", align_bytes=64)
            nc.vector.quantize_mx(
                out=e_codes[:].rearrange("p g n -> p (g n)").bitcast(FP8X4),
                scales=e_scales[:].rearrange("p g n -> p (g n)"),
                in_=live["e_grouped", i][:].rearrange("p g n t -> p (g n t)"),
            )
            live["e_codes", i] = e_codes
            live["e_scales", i] = e_scales

        def weighted_sum(i):
            pv_ps = psum.tile([P, C], F32, name="pv_ps", tag="pv")
            for g in range(KEY_PASSES):
                nc.tensor.matmul_mx(
                    out=pv_ps[:],
                    lhsT=live["e_codes", i][:, g, :].bitcast(FP8X4),
                    lhsT_scale=live["e_scales", i][:, g, :],
                    rhs=v_codes[:, g, :].bitcast(FP8X4),
                    rhs_scale=v_scales[:, g, :],
                    start=(g == 0),
                    stop=(g == KEY_PASSES - 1),
                )
            live["pv_ps", i] = pv_ps

        def normalise(i):
            matched = work.tile([P, C], BF16, name="matched", tag="matched")
            nc.scalar.activation(
                out=matched[:], in_=live["pv_ps", i][:], func=ACT.Copy, scale=live["e_inv", i][:, 0:1]
            )
            live["matched", i] = matched

        def transpose_matched(i, t_ps):
            m_words = live["matched", i][:].bitcast(F32)
            for u in range(2):
                nc.tensor.transpose(t_ps[:, 1, u, :], m_words[:, u * P : (u + 1) * P], ident_f32[:])

        def transpose_pair(i_q, i_m):
            tag, bufs = ("tqm", 1) if i_q < TILES else ("scores", 3)
            t_ps = psum.tile([P, 2, 2, P], F32, name="t_ps", tag=tag, bufs=bufs)
            if 0 <= i_m < TILES:
                transpose_matched(i_m, t_ps)
            if 0 <= i_q < TILES:
                transpose_queries(i_q, t_ps)
            live["t_ps", i_q] = t_ps

        def copy_pair(i_q, i_m):
            grouped = work.tile([P, 2, P, PACK], BF16, name="grouped", tag="grouped", align_bytes=64)
            parts = slice(0 if 0 <= i_q < TILES else 1, 2 if 0 <= i_m < TILES else 1)
            nc.scalar.copy(
                out=grouped[:].bitcast(F32)[:, parts], in_=live["t_ps", i_q][:].rearrange("p k u n -> p k n u")[:, parts]
            )
            live["qT", i_q] = grouped[:, 0]
            live["m_grouped", i_m] = grouped[:, 1]

        def quantise_matched(i):
            m_codes = work.tile([P, P], U32, name="m_codes", tag="m_codes", align_bytes=64)
            m_scales = work.tile([P, P], U8, name="m_scales", tag="m_scales", align_bytes=64)
            nc.vector.quantize_mx(
                out=m_codes[:].bitcast(FP8X4),
                scales=m_scales[:],
                in_=live["m_grouped", i].rearrange("p n t -> p (n t)"),
            )
            live["m_codes", i] = m_codes
            live["m_scales", i] = m_scales

        def project(i):
            o_ps = psum.tile([P, C], F32, name="o_ps", tag="fo", bufs=2)
            nc.tensor.matmul_mx(
                out=o_ps[:],
                lhsT=live["m_codes", i][:].bitcast(FP8X4),
                lhsT_scale=live["m_scales", i][:],
                rhs=w_codes[:].bitcast(FP8X4),
                rhs_scale=w_scales[:],
                start=True,
                stop=True,
            )
            live["o_ps", i] = o_ps

        def add_bias_and_store(i):
            o_rows = work.tile([P, C], F32, name="o_rows", tag="o_rows", bufs=4)
            nc.vector.tensor_tensor(out=o_rows[:], in0=live["o_ps", i][:], in1=bias_row[:], op=ALU.add)
            nc.sync.dma_start(out=out_view[:, i, :], in_=o_rows[:])

        def on_tile(stage, i, *args):
            if 0 <= i < TILES:
                stage(i, *args)

        def on_pair(stage, i_q, i_m):
            if 0 <= i_q < TILES or 0 <= i_m < TILES:
                stage(i_q, i_m)

        def step(k):
            on_tile(transpose_e, k - 2)
            on_pair(transpose_pair, k + 2, k - 5)
            on_tile(normalise, k - 4)
            on_tile(copy_e, k - 2)
            on_pair(copy_pair, k + 2, k - 5)
            on_tile(exponentials, k - 1)
            on_tile(mask_scores, k, 1)
            on_tile(quantise_matched, k - 6)
            on_tile(join_mask, k + 1)
            on_tile(add_bias_and_store, k - 7)
            on_tile(row_minimum, k)
            on_tile(mask_offset_v, k + 3)
            on_tile(exp_bias, k)
            on_tile(scores, k + 1, 0)
            on_tile(invert_sum, k - 2)
            on_tile(mask_distance_u, k + 3)
            on_tile(weighted_sum, k - 3)
            on_tile(project, k - 6)
            on_tile(mask_scores, k + 1, 0)
            on_tile(quantise_e, k - 2)
            on_tile(scores, k + 1, 1)

        for j, (tag, bufs) in enumerate((("fo", 2), ("fo", 2), ("te", 1), ("pv", 1))):
            broadcast_keys(j, tag, bufs, copied_by_vector=j < 1)
        mask_distance_u(0)
        for j in range(4):
            transpose_keys(j, "scores", 3)
        transpose_pair(0, -1)
        copy_pair(0, -1)
        mask_distance_u(1)
        for j in range(4, KEY_TILES):
            transpose_keys(j, "fo", 2)
        mask_offset_v(0)
        mask_offset_v(1)
        group_values(0, 0)
        group_values(0, 1)
        step(-1)
        transpose_weights(0)
        transpose_weights(1)
        group_values(1, 0)
        step(0)
        transpose_weights(2)
        transpose_weights(3)
        group_values(1, 1)
        step(1)
        step(2)
        quantise_values()
        quantise_weights()
        for k in range(3, TILES + 7):
            step(k)
